import numpy as np
import ml_dtypes

BF16 = ml_dtypes.bfloat16


def bf(x):
    return np.asarray(x, np.float32).astype(BF16)


def f32(x):
    return np.asarray(x, np.float32)


def f64(x):
    return np.asarray(x).astype(np.float64)


def striped(idx):
    return np.tile(idx.reshape(-1, 16).T, (8, 1))


MUL, DV, C, S, N = 128, 3, 512, 2048, 1024


def setup_inputs():
    return {
        "base": f32(np.random.standard_normal((C, S))),
        "scal": bf(np.random.standard_normal((MUL, N))),
        "vec": f32(np.random.standard_normal((DV * MUL, N))),
        "gate": f32(np.random.uniform(0.25, 1.75, (MUL, N))),
        "w0": bf(np.random.standard_normal((MUL, MUL))),
        "w1": bf(np.random.standard_normal((MUL, MUL))),
        "b": f32(0.1 * np.random.standard_normal((MUL, 1))),
        "pair_attr": f32(np.random.standard_normal((C, N))),
        "offs": striped(np.random.permutation(S)[:N]),
    }


def reference(base, scal, vec, gate, w0, w1, b, pair_attr, offs):
    idx = offs[:16].T.reshape(-1)
    gated = f64(vec).reshape(DV, MUL, N) * f64(gate)[None, :, :]
    lin0 = f64(w0).T @ f64(scal) / np.sqrt(MUL) + f64(b)
    lin1 = np.einsum("uv,iun->ivn", f64(w1), gated) / np.sqrt(MUL)
    upd = np.concatenate([lin0, lin1.reshape(DV * MUL, N)], axis=0) + f64(pair_attr)
    out = f64(base).copy()
    out[:, idx] = upd
    return out

@@ -1,0 +1,69 @@
+import math
+
+import concourse.mybir as mybir
+
+F32, BF16, U16 = mybir.dt.float32, mybir.dt.bfloat16, mybir.dt.uint16
+ADD, MULT = mybir.AluOpType.add, mybir.AluOpType.mult
+IDENTITY = mybir.ActivationFunctionType.Identity
+
+P = 128
+DV = 3
+BLOCKS = 1 + DV
+S = 2048
+N = 1024
+BANK = 512
+INV_SQRT_MUL = 1.0 / math.sqrt(P)
+
+FLOPS = 2 * BLOCKS * P * P * N
+
+
+def tile_pairnetlayer_symmetry_exp_kernel(tc, base, scal, vec, gate, w0, w1, b, pair_attr, offs, out):
+    nc = tc.nc
+    with (
+        tc.tile_pool(name="held", bufs=1) as held,
+        tc.psum_pool(name="banks", bufs=4) as banks,
+    ):
+        offsets = held.tile([P, N // 16], U16, name="offsets")
+        scalars = held.tile([P, N], BF16, name="scalars")
+        weights0 = held.tile([P, P], BF16, name="weights0")
+        weights1 = held.tile([P, P], BF16, name="weights1")
+        bias = held.tile([P, 1], F32, name="bias")
+        gates = held.tile([P, N], F32, name="gates")
+        vectors = [held.tile([P, N], F32, name=f"vectors{i}") for i in range(DV)]
+        gated = [held.tile([P, N], BF16, name=f"gated{i}") for i in range(DV)]
+        windows = [held.tile([P, S], F32, name=f"window{k}") for k in range(BLOCKS)]
+        residuals = [held.tile([P, N], F32, name=f"residual{k}") for k in range(BLOCKS)]
+        mixed = [held.tile([P, N], F32, name=f"mixed{k}") for k in range(BLOCKS)]
+
+        def rows(dram, k):
+            return dram[k * P : (k + 1) * P, :]
+
+        nc.sync.dma_start(offsets[:], offs)
+        nc.sync.dma_start(scalars[:], scal)
+        nc.sync.dma_start(weights0[:], w0)
+        nc.sync.dma_start(bias[:], b)
+        nc.sync.dma_start(windows[0][:], rows(base, 0))
+        nc.sync.dma_start(residuals[0][:], rows(pair_attr, 0))
+        nc.sync.dma_start(gates[:], gate)
+        nc.sync.dma_start(weights1[:], w1)
+        for i in range(DV):
+            nc.sync.dma_start(vectors[i][:], rows(vec, i))
+        for k in range(1, BLOCKS):
+            nc.sync.dma_start(windows[k][:], rows(base, k))
+            nc.sync.dma_start(residuals[k][:], rows(pair_attr, k))
+
+        def update(k, weights, moving, shift):
+            for h in range(N // BANK):
+                bank = banks.tile([P, BANK], F32, name="bank")
+                nc.tensor.matmul(bank[:], weights[:], moving[:, h * BANK : (h + 1) * BANK], start=True, stop=True)
+                nc.scalar.activation(
+                    mixed[k][:, h * BANK : (h + 1) * BANK], bank[:], IDENTITY, bias=shift, scale=INV_SQRT_MUL
+                )
+            nc.vector.tensor_tensor(windows[k][:].indirect(offsets[:]), mixed[k][:], residuals[k][:], ADD)
+            nc.sync.dma_start(rows(out, k), windows[k][:])
+
+        update(0, weights0, scalars, bias[:])
+        for i in range(DV):
+            nc.vector.tensor_tensor(gated[i][:], vectors[i][:], gates[:], MULT)
+        for i in range(DV):
+            update(1 + i, weights1, gated[i], 0.0)

@@ -64,6 +64,6 @@ def tile_pairnetlayer_symmetry_exp_kernel(tc, base, scal, vec, gate, w0, w1, b, 
 
         update(0, weights0, scalars, bias[:])
         for i in range(DV):
-            nc.vector.tensor_tensor(gated[i][:], vectors[i][:], gates[:], MULT)
+            nc.gpsimd.tensor_tensor(gated[i][:], vectors[i][:], gates[:], MULT)
         for i in range(DV):
             update(1 + i, weights1, gated[i], 0.0)

@@ -35,6 +35,10 @@ def tile_pairnetlayer_symmetry_exp_kernel(tc, base, scal, vec, gate, w0, w1, b, 
         residuals = [held.tile([P, N], F32, name=f"residual{k}") for k in range(BLOCKS)]
         mixed = [held.tile([P, N], F32, name=f"mixed{k}") for k in range(BLOCKS)]
 
+        scratch = held.tile([P, 1], F32, name="scratch")
+        nc.vector.memset(scratch[:], 0.0)
+        nc.scalar.activation(scratch[:], scratch[:], IDENTITY)
+
         def rows(dram, k):
             return dram[k * P : (k + 1) * P, :]
 
@@ -64,6 +68,6 @@ def tile_pairnetlayer_symmetry_exp_kernel(tc, base, scal, vec, gate, w0, w1, b, 
 
         update(0, weights0, scalars, bias[:])
         for i in range(DV):
-            nc.gpsimd.tensor_tensor(gated[i][:], vectors[i][:], gates[:], MULT)
+            nc.vector.tensor_tensor(gated[i][:], vectors[i][:], gates[:], MULT)
         for i in range(DV):
             update(1 + i, weights1, gated[i], 0.0)

@@ -35,10 +35,6 @@ def tile_pairnetlayer_symmetry_exp_kernel(tc, base, scal, vec, gate, w0, w1, b, 
         residuals = [held.tile([P, N], F32, name=f"residual{k}") for k in range(BLOCKS)]
         mixed = [held.tile([P, N], F32, name=f"mixed{k}") for k in range(BLOCKS)]
 
-        scratch = held.tile([P, 1], F32, name="scratch")
-        nc.vector.memset(scratch[:], 0.0)
-        nc.scalar.activation(scratch[:], scratch[:], IDENTITY)
-
         def rows(dram, k):
             return dram[k * P : (k + 1) * P, :]
 
@@ -68,6 +64,8 @@ def tile_pairnetlayer_symmetry_exp_kernel(tc, base, scal, vec, gate, w0, w1, b, 
 
         update(0, weights0, scalars, bias[:])
         for i in range(DV):
-            nc.vector.tensor_tensor(gated[i][:], vectors[i][:], gates[:], MULT)
+            for h in range(N // BANK):
+                cols = slice(h * BANK, (h + 1) * BANK)
+                nc.vector.tensor_tensor(gated[i][:, cols], vectors[i][:, cols], gates[:, cols], MULT)
         for i in range(DV):
             update(1 + i, weights1, gated[i], 0.0)

@@ -1,6 +1,7 @@
 import math
 
 import concourse.mybir as mybir
+from concourse.masks import make_identity
 
 F32, BF16, U16 = mybir.dt.float32, mybir.dt.bfloat16, mybir.dt.uint16
 ADD, MULT = mybir.AluOpType.add, mybir.AluOpType.mult
@@ -22,6 +23,7 @@ def tile_pairnetlayer_symmetry_exp_kernel(tc, base, scal, vec, gate, w0, w1, b, 
     with (
         tc.tile_pool(name="held", bufs=1) as held,
         tc.psum_pool(name="banks", bufs=4) as banks,
+        tc.psum_pool(name="gate_banks", bufs=1) as gate_banks,
     ):
         offsets = held.tile([P, N // 16], U16, name="offsets")
         scalars = held.tile([P, N], BF16, name="scalars")
@@ -29,11 +31,15 @@ def tile_pairnetlayer_symmetry_exp_kernel(tc, base, scal, vec, gate, w0, w1, b, 
         weights1 = held.tile([P, P], BF16, name="weights1")
         bias = held.tile([P, 1], F32, name="bias")
         gates = held.tile([P, N], F32, name="gates")
+        identity = held.tile([P, P], F32, name="identity")
+        gates_psum = [gate_banks.tile([P, BANK], F32, name=f"gates_psum{h}") for h in range(N // BANK)]
         vectors = [held.tile([P, N], F32, name=f"vectors{i}") for i in range(DV)]
         gated = [held.tile([P, N], BF16, name=f"gated{i}") for i in range(DV)]
         windows = [held.tile([P, S], F32, name=f"window{k}") for k in range(BLOCKS)]
         residuals = [held.tile([P, N], F32, name=f"residual{k}") for k in range(BLOCKS)]
         mixed = [held.tile([P, N], F32, name=f"mixed{k}") for k in range(BLOCKS)]
+
+        make_identity(nc, identity[:])
 
         def rows(dram, k):
             return dram[k * P : (k + 1) * P, :]
@@ -63,9 +69,12 @@ def tile_pairnetlayer_symmetry_exp_kernel(tc, base, scal, vec, gate, w0, w1, b, 
             nc.sync.dma_start(rows(out, k), windows[k][:])
 
         update(0, weights0, scalars, bias[:])
-        for i in range(DV):
+        for h in range(N // BANK):
+            nc.tensor.matmul(gates_psum[h][:], identity[:], gates[:, h * BANK : (h + 1) * BANK], start=True, stop=True)
+        nc.gpsimd.tensor_tensor(gated[DV - 1][:], vectors[DV - 1][:], gates[:], MULT)
+        for i in range(DV - 1):
             for h in range(N // BANK):
                 cols = slice(h * BANK, (h + 1) * BANK)
-                nc.vector.tensor_tensor(gated[i][:, cols], vectors[i][:, cols], gates[:, cols], MULT)
+                nc.vector.tensor_tensor(gated[i][:, cols], vectors[i][:, cols], gates_psum[h][:], MULT)
         for i in range(DV):
             update(1 + i, weights1, gated[i], 0.0)

@@ -58,23 +58,24 @@ def tile_pairnetlayer_symmetry_exp_kernel(tc, base, scal, vec, gate, w0, w1, b, 
             nc.sync.dma_start(windows[k][:], rows(base, k))
             nc.sync.dma_start(residuals[k][:], rows(pair_attr, k))
 
-        def update(k, weights, moving, shift):
-            for h in range(N // BANK):
+        def update(k, weights, moving, shift, width):
+            for first in range(0, N, width):
+                cols = slice(first, first + width)
                 bank = banks.tile([P, BANK], F32, name="bank")
-                nc.tensor.matmul(bank[:], weights[:], moving[:, h * BANK : (h + 1) * BANK], start=True, stop=True)
-                nc.scalar.activation(
-                    mixed[k][:, h * BANK : (h + 1) * BANK], bank[:], IDENTITY, bias=shift, scale=INV_SQRT_MUL
-                )
+                nc.tensor.matmul(bank[:, :width], weights[:], moving[:, cols], start=True, stop=True)
+                nc.scalar.activation(mixed[k][:, cols], bank[:, :width], IDENTITY, bias=shift, scale=INV_SQRT_MUL)
             nc.vector.tensor_tensor(windows[k][:].indirect(offsets[:]), mixed[k][:], residuals[k][:], ADD)
             nc.sync.dma_start(rows(out, k), windows[k][:])
 
-        update(0, weights0, scalars, bias[:])
+        update(0, weights0, scalars, bias[:], BANK)
         for h in range(N // BANK):
             nc.tensor.matmul(gates_psum[h][:], identity[:], gates[:, h * BANK : (h + 1) * BANK], start=True, stop=True)
+        widths = [BANK // 2, BANK, BANK]
         nc.gpsimd.tensor_tensor(gated[DV - 1][:], vectors[DV - 1][:], gates[:], MULT)
         for i in range(DV - 1):
-            for h in range(N // BANK):
-                cols = slice(h * BANK, (h + 1) * BANK)
-                nc.vector.tensor_tensor(gated[i][:, cols], vectors[i][:, cols], gates_psum[h][:], MULT)
+            for first in range(0, N, widths[i]):
+                cols = slice(first, first + widths[i])
+                in_bank = slice(first % BANK, first % BANK + widths[i])
+                nc.vector.tensor_tensor(gated[i][:, cols], vectors[i][:, cols], gates_psum[first // BANK][:, in_bank], MULT)
         for i in range(DV):
-            update(1 + i, weights1, gated[i], 0.0)
+            update(1 + i, weights1, gated[i], 0.0, widths[i])

@@ -70,7 +70,7 @@ def tile_pairnetlayer_symmetry_exp_kernel(tc, base, scal, vec, gate, w0, w1, b, 
         update(0, weights0, scalars, bias[:], BANK)
         for h in range(N // BANK):
             nc.tensor.matmul(gates_psum[h][:], identity[:], gates[:, h * BANK : (h + 1) * BANK], start=True, stop=True)
-        widths = [BANK // 2, BANK, BANK]
+        widths = [BANK // 4, BANK, BANK]
         nc.gpsimd.tensor_tensor(gated[DV - 1][:], vectors[DV - 1][:], gates[:], MULT)
         for i in range(DV - 1):
             for first in range(0, N, widths[i]):

@@ -46,8 +46,8 @@ def tile_pairnetlayer_symmetry_exp_kernel(tc, base, scal, vec, gate, w0, w1, b, 
 
         nc.sync.dma_start(offsets[:], offs)
         nc.sync.dma_start(scalars[:], scal)
-        nc.sync.dma_start(weights0[:], w0)
-        nc.sync.dma_start(bias[:], b)
+        nc.scalar.dma_start(weights0[:], w0)
+        nc.scalar.dma_start(bias[:], b)
         nc.sync.dma_start(windows[0][:], rows(base, 0))
         nc.sync.dma_start(residuals[0][:], rows(pair_attr, 0))
         nc.sync.dma_start(gates[:], gate)

@@ -13,6 +13,7 @@ BLOCKS = 1 + DV
 S = 2048
 N = 1024
 BANK = 512
+LENT = N // 16
 INV_SQRT_MUL = 1.0 / math.sqrt(P)
 
 FLOPS = 2 * BLOCKS * P * P * N
@@ -70,12 +71,17 @@ def tile_pairnetlayer_symmetry_exp_kernel(tc, base, scal, vec, gate, w0, w1, b, 
         update(0, weights0, scalars, bias[:], BANK)
         for h in range(N // BANK):
             nc.tensor.matmul(gates_psum[h][:], identity[:], gates[:, h * BANK : (h + 1) * BANK], start=True, stop=True)
-        widths = [BANK // 4, BANK, BANK]
-        nc.gpsimd.tensor_tensor(gated[DV - 1][:], vectors[DV - 1][:], gates[:], MULT)
+        widths = [BANK // 2, BANK, BANK]
+
+        def gate_on_vector(i, first, width):
+            cols = slice(first, first + width)
+            in_bank = slice(first % BANK, first % BANK + width)
+            nc.vector.tensor_tensor(gated[i][:, cols], vectors[i][:, cols], gates_psum[first // BANK][:, in_bank], MULT)
+
+        nc.gpsimd.tensor_tensor(gated[DV - 1][:, LENT:], vectors[DV - 1][:, LENT:], gates[:, LENT:], MULT)
         for i in range(DV - 1):
             for first in range(0, N, widths[i]):
-                cols = slice(first, first + widths[i])
-                in_bank = slice(first % BANK, first % BANK + widths[i])
-                nc.vector.tensor_tensor(gated[i][:, cols], vectors[i][:, cols], gates_psum[first // BANK][:, in_bank], MULT)
+                gate_on_vector(i, first, widths[i])
+        gate_on_vector(DV - 1, 0, LENT)
         for i in range(DV):
             update(1 + i, weights1, gated[i], 0.0, widths[i])

@@ -36,9 +36,11 @@ def tile_pairnetlayer_symmetry_exp_kernel(tc, base, scal, vec, gate, w0, w1, b, 
         gates_psum = [gate_banks.tile([P, BANK], F32, name=f"gates_psum{h}") for h in range(N // BANK)]
         vectors = [held.tile([P, N], F32, name=f"vectors{i}") for i in range(DV)]
         gated = [held.tile([P, N], BF16, name=f"gated{i}") for i in range(DV)]
-        windows = [held.tile([P, S], F32, name=f"window{k}") for k in range(BLOCKS)]
-        residuals = [held.tile([P, N], F32, name=f"residual{k}") for k in range(BLOCKS)]
-        mixed = [held.tile([P, N], F32, name=f"mixed{k}") for k in range(BLOCKS)]
+        windows, residuals, mixed = [], [], []
+        for k in range(BLOCKS):
+            windows.append(held.tile([P, S], F32, name=f"window{k}"))
+            residuals.append(held.tile([P, N], F32, name=f"residual{k}"))
+            mixed.append(held.tile([P, N], F32, name=f"mixed{k}"))
 
         make_identity(nc, identity[:])
 

@@ -5,7 +5,7 @@ from concourse.masks import make_identity
 
 F32, BF16, U16 = mybir.dt.float32, mybir.dt.bfloat16, mybir.dt.uint16
 ADD, MULT = mybir.AluOpType.add, mybir.AluOpType.mult
-IDENTITY = mybir.ActivationFunctionType.Identity
+COPY, IDENTITY = mybir.ActivationFunctionType.Copy, mybir.ActivationFunctionType.Identity
 
 P = 128
 DV = 3
@@ -61,14 +61,20 @@ def tile_pairnetlayer_symmetry_exp_kernel(tc, base, scal, vec, gate, w0, w1, b, 
             nc.sync.dma_start(windows[k][:], rows(base, k))
             nc.sync.dma_start(residuals[k][:], rows(pair_attr, k))
 
-        def update(k, weights, moving, shift, width):
-            for first in range(0, N, width):
-                cols = slice(first, first + width)
+        def update(k, weights, moving, shift, piece):
+            for first in range(0, N, piece):
+                cols = slice(first, first + piece)
                 bank = banks.tile([P, BANK], F32, name="bank")
-                nc.tensor.matmul(bank[:, :width], weights[:], moving[:, cols], start=True, stop=True)
-                nc.scalar.activation(mixed[k][:, cols], bank[:, :width], IDENTITY, bias=shift, scale=INV_SQRT_MUL)
+                nc.tensor.matmul(bank[:, :piece], weights[:], moving[:, cols], start=True, stop=True)
+                if shift is None:
+                    nc.scalar.activation(mixed[k][:, cols], bank[:, :piece], COPY, scale=INV_SQRT_MUL)
+                else:
+                    nc.scalar.activation(mixed[k][:, cols], bank[:, :piece], IDENTITY, bias=shift, scale=INV_SQRT_MUL)
             nc.vector.tensor_tensor(windows[k][:].indirect(offsets[:]), mixed[k][:], residuals[k][:], ADD)
-            nc.sync.dma_start(rows(out, k), windows[k][:])
+            width = S if k == BLOCKS - 1 else S // 2
+            for first in range(0, S, width):
+                cols = slice(first, first + width)
+                nc.sync.dma_start(rows(out, k)[:, cols], windows[k][:, cols])
 
         update(0, weights0, scalars, bias[:], BANK)
         for h in range(N // BANK):
@@ -86,4 +92,4 @@ def tile_pairnetlayer_symmetry_exp_kernel(tc, base, scal, vec, gate, w0, w1, b, 
                 gate_on_vector(i, first, widths[i])
         gate_on_vector(DV - 1, 0, LENT)
         for i in range(DV):
-            update(1 + i, weights1, gated[i], 0.0, widths[i])
+            update(1 + i, weights1, gated[i], None, widths[i])

import math

import concourse.mybir as mybir
from concourse.masks import make_identity

F32, BF16, U16 = mybir.dt.float32, mybir.dt.bfloat16, mybir.dt.uint16
ADD, MULT = mybir.AluOpType.add, mybir.AluOpType.mult
COPY, IDENTITY = mybir.ActivationFunctionType.Copy, mybir.ActivationFunctionType.Identity

P = 128
DV = 3
BLOCKS = 1 + DV
S = 2048
N = 1024
BANK = 512
LENT = N // 16
INV_SQRT_MUL = 1.0 / math.sqrt(P)

FLOPS = 2 * BLOCKS * P * P * N


def tile_pairnetlayer_symmetry_exp_kernel(tc, base, scal, vec, gate, w0, w1, b, pair_attr, offs, out):
    nc = tc.nc
    with (
        tc.tile_pool(name="held", bufs=1) as held,
        tc.psum_pool(name="banks", bufs=4) as banks,
        tc.psum_pool(name="gate_banks", bufs=1) as gate_banks,
    ):
        offsets = held.tile([P, N // 16], U16, name="offsets")
        scalars = held.tile([P, N], BF16, name="scalars")
        weights0 = held.tile([P, P], BF16, name="weights0")
        weights1 = held.tile([P, P], BF16, name="weights1")
        bias = held.tile([P, 1], F32, name="bias")
        gates = held.tile([P, N], F32, name="gates")
        identity = held.tile([P, P], F32, name="identity")
        gates_psum = [gate_banks.tile([P, BANK], F32, name=f"gates_psum{h}") for h in range(N // BANK)]
        vectors = [held.tile([P, N], F32, name=f"vectors{i}") for i in range(DV)]
        gated = [held.tile([P, N], BF16, name=f"gated{i}") for i in range(DV)]
        windows, residuals, mixed = [], [], []
        for k in range(BLOCKS):
            windows.append(held.tile([P, S], F32, name=f"window{k}"))
            residuals.append(held.tile([P, N], F32, name=f"residual{k}"))
            mixed.append(held.tile([P, N], F32, name=f"mixed{k}"))

        make_identity(nc, identity[:])

        def rows(dram, k):
            return dram[k * P : (k + 1) * P, :]

        nc.sync.dma_start(offsets[:], offs)
        nc.sync.dma_start(scalars[:], scal)
        nc.scalar.dma_start(weights0[:], w0)
        nc.scalar.dma_start(bias[:], b)
        nc.sync.dma_start(windows[0][:], rows(base, 0))
        nc.sync.dma_start(residuals[0][:], rows(pair_attr, 0))
        nc.sync.dma_start(gates[:], gate)
        nc.sync.dma_start(weights1[:], w1)
        for i in range(DV):
            nc.sync.dma_start(vectors[i][:], rows(vec, i))
        for k in range(1, BLOCKS):
            nc.sync.dma_start(windows[k][:], rows(base, k))
            nc.sync.dma_start(residuals[k][:], rows(pair_attr, k))

        def update(k, weights, moving, shift, piece):
            for first in range(0, N, piece):
                cols = slice(first, first + piece)
                bank = banks.tile([P, BANK], F32, name="bank")
                nc.tensor.matmul(bank[:, :piece], weights[:], moving[:, cols], start=True, stop=True)
                if shift is None:
                    nc.scalar.activation(mixed[k][:, cols], bank[:, :piece], COPY, scale=INV_SQRT_MUL)
                else:
                    nc.scalar.activation(mixed[k][:, cols], bank[:, :piece], IDENTITY, bias=shift, scale=INV_SQRT_MUL)
            nc.vector.tensor_tensor(windows[k][:].indirect(offsets[:]), mixed[k][:], residuals[k][:], ADD)
            width = S if k == BLOCKS - 1 else S // 2
            for first in range(0, S, width):
                cols = slice(first, first + width)
                nc.sync.dma_start(rows(out, k)[:, cols], windows[k][:, cols])

        update(0, weights0, scalars, bias[:], BANK)
        for h in range(N // BANK):
            nc.tensor.matmul(gates_psum[h][:], identity[:], gates[:, h * BANK : (h + 1) * BANK], start=True, stop=True)
        widths = [BANK // 2, BANK, BANK]

        def gate_on_vector(i, first, width):
            cols = slice(first, first + width)
            in_bank = slice(first % BANK, first % BANK + width)
            nc.vector.tensor_tensor(gated[i][:, cols], vectors[i][:, cols], gates_psum[first // BANK][:, in_bank], MULT)

        nc.gpsimd.tensor_tensor(gated[DV - 1][:, LENT:], vectors[DV - 1][:, LENT:], gates[:, LENT:], MULT)
        for i in range(DV - 1):
            for first in range(0, N, widths[i]):
                gate_on_vector(i, first, widths[i])
        gate_on_vector(DV - 1, 0, LENT)
        for i in range(DV):
            update(1 + i, weights1, gated[i], None, widths[i])
